import numpy as np
import ml_dtypes


def mxq(x, axis, fmt="e4m3"):
    dtype, down = {"e4m3": (ml_dtypes.float8_e4m3fn, 7), "e5m2": (ml_dtypes.float8_e5m2, 14)}[fmt]
    v = np.moveaxis(np.asarray(x, np.float32).astype(ml_dtypes.bfloat16).astype(np.float64), axis, -1)
    blocks = v.reshape(v.shape[:-1] + (-1, 32))
    amax = np.abs(blocks).max(-1, keepdims=True)
    byte = np.maximum(np.where(amax > 0, np.frexp(amax)[1] - 1 + 127, 0) - down, 1)
    scale = np.exp2(byte - 127.0)
    codes = (blocks / scale).astype(np.float32).astype(dtype).astype(np.float64)
    return np.moveaxis((codes * scale).reshape(v.shape), -1, axis)


WIDE = False


def mx_kscale(k):
    if not WIDE:
        return np.ones(k)
    levels = np.array([10, -10, 5, -5, 0])
    a = np.random.permutation(np.resize(levels, k // 512 * 4)).reshape(k // 512, 4)
    idx = np.arange(k)
    return np.exp2(a[idx // 512, idx % 128 // 32])


BF16 = ml_dtypes.bfloat16


def bf(x):
    return np.asarray(x, np.float32).astype(BF16)


def f64(x):
    return np.asarray(x).astype(np.float64)


B, S, H = 8, 129, 1024
N = B * (S - 1)
G = 0.75


def setup_inputs():
    s = mx_kscale(H)
    return {"x": bf(np.random.standard_normal((B, S, H)) * s),
            "k1": bf(np.random.standard_normal((N, H)) * G * s),
            "k2": bf(np.random.standard_normal((N, H)) * G * np.sqrt(1.0 + 0.25 * G * G) * s),
            "coefficients": bf(np.random.standard_normal((H, H)) * G / np.sqrt(H) * s[:, None] / s[None, :])}


def reference(x, k1, k2, coefficients):
    x, k1, k2 = f64(x), f64(k1), f64(k2)
    y = x[:, :-1, :].reshape(-1, H)
    cq = mxq(f64(coefficients), 1, "e4m3")
    k3 = mxq(y + 0.5 * k2, 1, "e4m3") @ cq.T
    k4 = mxq(y + k3, 1, "e4m3") @ cq.T
    y1 = y + (k1 + 2.0 * k2 + 2.0 * k3 + k4) / 6.0
    return y1.reshape(B, S - 1, H) - x[:, 1:, :]

@@ -1,0 +1,181 @@
+from contextlib import ExitStack
+
+import concourse.mybir as mybir
+from concourse.masks import make_identity
+
+BF16 = mybir.dt.bfloat16
+F32 = mybir.dt.float32
+U32 = mybir.dt.uint32
+U8 = mybir.dt.uint8
+FP8X4 = mybir.dt.float8_e4m3fn_x4
+ADD = mybir.AluOpType.add
+SUBTRACT = mybir.AluOpType.subtract
+MULT = mybir.AluOpType.mult
+COPY = mybir.ActivationFunctionType.Copy
+
+P = 128
+PACK = 4
+K_PASS = P * PACK
+H = 1024
+PASSES = H // K_PASS
+BANK = 512
+HALVES = H // BANK
+ROW_TILES = 8
+
+FLOPS = 2 * 2 * (ROW_TILES * P) * H * H
+
+
+def tile_sindylossmixin_pa_kernel(tc, x, k1, k2, coefficients, out):
+    nc = tc.nc
+    with ExitStack() as stack:
+        keep = stack.enter_context(tc.tile_pool(name="keep", bufs=1))
+        work = stack.enter_context(tc.tile_pool(name="work", bufs=3))
+        turned_banks = stack.enter_context(tc.psum_pool(name="turned_banks", bufs=4))
+        product_banks = stack.enter_context(tc.psum_pool(name="product_banks", bufs=4))
+
+        identity_bf16 = keep.tile([P, P], BF16)
+        make_identity(nc, identity_bf16[:])
+        identity_f32 = keep.tile([P, P], F32)
+        make_identity(nc, identity_f32[:])
+
+        y, x_next, k1_rows, k2_rows, c_rows = [], [], [], [], []
+        for t in range(ROW_TILES):
+            y.append(keep.tile([P, H], BF16, name="y%d" % t))
+            x_next.append(keep.tile([P, H], BF16, name="x_next%d" % t))
+            k1_rows.append(keep.tile([P, H], BF16, name="k1_rows%d" % t))
+            k2_rows.append(keep.tile([P, H], BF16, name="k2_rows%d" % t))
+            c_rows.append(keep.tile([P, H], BF16, name="c_rows%d" % t))
+
+        def load_first_argument(t):
+            nc.sync.dma_start(out=y[t][:], in_=x[t, 0:P, :])
+            nc.sync.dma_start(out=k2_rows[t][:], in_=k2[t * P : (t + 1) * P, :])
+
+        def load_rest(t):
+            nc.sync.dma_start(out=k1_rows[t][:], in_=k1[t * P : (t + 1) * P, :])
+            nc.sync.dma_start(out=x_next[t][:], in_=x[t, 1 : P + 1, :])
+
+        load_first_argument(0)
+        for r in range(ROW_TILES):
+            nc.sync.dma_start(out=c_rows[r][:], in_=coefficients[r * P : (r + 1) * P, :])
+        for t in range(1, ROW_TILES):
+            load_first_argument(t)
+            load_rest(t - 1)
+        load_rest(ROW_TILES - 1)
+
+        c_grouped = keep.tile([P, PASSES, H, PACK], BF16, align_bytes=64)
+        c_codes = keep.tile([P, PASSES, H], U32, align_bytes=64)
+        c_scales = keep.tile([P, PASSES, H], U8, align_bytes=64)
+        tiles_per_half = BANK // P
+        for r in range(ROW_TILES):
+            rows = slice(r * P, (r + 1) * P)
+            for g in range(PASSES):
+                turned = turned_banks.tile([P, PACK, P], BF16, tag="turned")
+                for j in range(PACK):
+                    k_cols = slice(g * K_PASS + j * P, g * K_PASS + (j + 1) * P)
+                    nc.tensor.transpose(turned[:, j, :], c_rows[r][:, k_cols], identity_bf16[:])
+                copy_out = nc.vector.tensor_copy if g == 0 else nc.scalar.copy
+                copy_out(out=c_grouped[:, g, rows, :], in_=turned[:].rearrange("p j i -> p i j"))
+            if (r + 1) % tiles_per_half == 0:
+                half = slice((r + 1) * P - BANK, (r + 1) * P)
+                for g in range(PASSES):
+                    nc.vector.quantize_mx(
+                        out=c_codes[:, g, half].bitcast(FP8X4),
+                        scales=c_scales[:, g, half],
+                        in_=c_grouped[:, g, half, :].rearrange("p i j -> p (i j)"),
+                    )
+
+        def quantise_argument(argument, scale, label):
+            grouped = work.tile([P, PASSES, P, PACK], BF16, tag="grouped_" + label, align_bytes=64)
+            for g in range(PASSES):
+                turned = turned_banks.tile([P, PACK, P], F32, tag="turned")
+                for j in range(PACK):
+                    k_cols = slice(g * K_PASS + j * P, g * K_PASS + (j + 1) * P)
+                    nc.tensor.transpose(turned[:, j, :], argument[:, k_cols], identity_f32[:])
+                nc.scalar.activation(
+                    out=grouped[:, g, :, :],
+                    in_=turned[:].rearrange("p j n -> p n j"),
+                    func=COPY,
+                    scale=scale,
+                )
+            codes = work.tile([P, PASSES, P], U32, tag="codes_" + label, align_bytes=64)
+            scales = work.tile([P, PASSES, P], U8, tag="scales_" + label, align_bytes=64)
+            nc.vector.quantize_mx(
+                out=codes[:].rearrange("p g n -> p (g n)").bitcast(FP8X4),
+                scales=scales[:].rearrange("p g n -> p (g n)"),
+                in_=grouped[:].rearrange("p g n j -> p (g n j)"),
+            )
+            return codes, scales
+
+        def times_coefficients(codes, scales, h):
+            cols = slice(h * BANK, (h + 1) * BANK)
+            product = product_banks.tile([P, BANK], F32, tag="product")
+            for g in range(PASSES):
+                nc.tensor.matmul_mx(
+                    out=product[:],
+                    lhsT=codes[:, g, :].bitcast(FP8X4),
+                    lhsT_scale=scales[:, g, :],
+                    rhs=c_codes[:, g, cols].bitcast(FP8X4),
+                    rhs_scale=c_scales[:, g, cols],
+                    start=(g == 0),
+                    stop=(g == PASSES - 1),
+                )
+            return product
+
+        doubled_a, a_quantised, b_plus_a, b_quantised = {}, {}, {}, {}
+
+        def first_argument(t):
+            doubled_a[t] = work.tile([P, H], F32, name="doubled_a")
+            nc.vector.scalar_tensor_tensor(
+                out=doubled_a[t][:], in0=y[t][:], scalar=2.0, in1=k2_rows[t][:], op0=MULT, op1=ADD
+            )
+            a_quantised[t] = quantise_argument(doubled_a[t], 0.5, "a")
+
+        def first_product(t):
+            codes, scales = a_quantised[t]
+            b = work.tile([P, H], F32, name="b")
+            for h in range(HALVES):
+                cols = slice(h * BANK, (h + 1) * BANK)
+                k3 = times_coefficients(codes, scales, h)
+                nc.vector.tensor_tensor(out=b[:, cols], in0=k3[:], in1=y[t][:, cols], op=ADD)
+            b_quantised[t] = quantise_argument(b, 1.0, "b")
+            b_plus_a[t] = work.tile([P, H], F32, name="b_plus_a")
+            nc.gpsimd.tensor_tensor(out=b_plus_a[t][:], in0=b[:], in1=doubled_a[t][:], op=ADD)
+
+        def second_product(t):
+            k1_sixth = work.tile([P, H], F32, name="k1_sixth")
+            nc.scalar.activation(out=k1_sixth[:], in_=k1_rows[t][:], func=COPY, scale=1.0 / 6.0)
+            from_inputs = work.tile([P, H], F32, name="from_inputs")
+            nc.gpsimd.tensor_tensor(
+                out=from_inputs[:], in0=k1_sixth[:], in1=x_next[t][:], op=SUBTRACT
+            )
+            all_but_k4 = work.tile([P, H], F32, name="all_but_k4")
+            nc.vector.scalar_tensor_tensor(
+                out=all_but_k4[:],
+                in0=b_plus_a[t][:],
+                scalar=1.0 / 3.0,
+                in1=from_inputs[:],
+                op0=MULT,
+                op1=ADD,
+            )
+            codes, scales = b_quantised[t]
+            result = work.tile([P, H], F32, name="result")
+            for h in range(HALVES):
+                cols = slice(h * BANK, (h + 1) * BANK)
+                k4 = times_coefficients(codes, scales, h)
+                nc.vector.scalar_tensor_tensor(
+                    out=result[:, cols],
+                    in0=k4[:],
+                    scalar=1.0 / 6.0,
+                    in1=all_but_k4[:, cols],
+                    op0=MULT,
+                    op1=ADD,
+                )
+                nc.sync.dma_start(out=out[t, :, cols], in_=result[:, cols])
+
+        for step in range(ROW_TILES + 2):
+            if 0 <= step - 2:
+                second_product(step - 2)
+            if 0 <= step - 1 < ROW_TILES:
+                first_product(step - 1)
+            if step < ROW_TILES:
+                first_argument(step)

@@ -22,12 +22,17 @@ BANK = 512
 HALVES = H // BANK
 ROW_TILES = 8
 
+A_AHEAD = 2
+B_BEHIND = 1
+OUT_BEHIND = 2
+
 FLOPS = 2 * 2 * (ROW_TILES * P) * H * H
 
 
 def tile_sindylossmixin_pa_kernel(tc, x, k1, k2, coefficients, out):
     nc = tc.nc
     with ExitStack() as stack:
+        stack.enter_context(tc.manual_schedule())
         keep = stack.enter_context(tc.tile_pool(name="keep", bufs=1))
         work = stack.enter_context(tc.tile_pool(name="work", bufs=3))
         turned_banks = stack.enter_context(tc.psum_pool(name="turned_banks", bufs=4))
@@ -84,98 +89,120 @@ def tile_sindylossmixin_pa_kernel(tc, x, k1, k2, coefficients, out):
                         in_=c_grouped[:, g, half, :].rearrange("p i j -> p (i j)"),
                     )
 
-        def quantise_argument(argument, scale, label):
-            grouped = work.tile([P, PASSES, P, PACK], BF16, tag="grouped_" + label, align_bytes=64)
+        doubled_a, b, b_plus_a, total = {}, {}, {}, {}
+        grouped, quantised, product = {}, {}, {}
+
+        def compute_first_argument(t):
+            doubled_a[t] = work.tile([P, H], F32, name="doubled_a", bufs=A_AHEAD + B_BEHIND + 2)
+            nc.vector.scalar_tensor_tensor(
+                out=doubled_a[t][:], in0=y[t][:], scalar=2.0, in1=k2_rows[t][:], op0=MULT, op1=ADD
+            )
+
+        def turn(label, argument, scale, t):
+            grouped[label, t] = work.tile(
+                [P, PASSES, P, PACK], BF16, name="grouped_" + label, align_bytes=64
+            )
             for g in range(PASSES):
                 turned = turned_banks.tile([P, PACK, P], F32, tag="turned")
                 for j in range(PACK):
                     k_cols = slice(g * K_PASS + j * P, g * K_PASS + (j + 1) * P)
                     nc.tensor.transpose(turned[:, j, :], argument[:, k_cols], identity_f32[:])
                 nc.scalar.activation(
-                    out=grouped[:, g, :, :],
+                    out=grouped[label, t][:, g, :, :],
                     in_=turned[:].rearrange("p j n -> p n j"),
                     func=COPY,
                     scale=scale,
                 )
-            codes = work.tile([P, PASSES, P], U32, tag="codes_" + label, align_bytes=64)
-            scales = work.tile([P, PASSES, P], U8, tag="scales_" + label, align_bytes=64)
+
+        def quantise(label, t):
+            codes = work.tile([P, PASSES, P], U32, name="codes_" + label, align_bytes=64)
+            scales = work.tile([P, PASSES, P], U8, name="scales_" + label, align_bytes=64)
             nc.vector.quantize_mx(
                 out=codes[:].rearrange("p g n -> p (g n)").bitcast(FP8X4),
                 scales=scales[:].rearrange("p g n -> p (g n)"),
-                in_=grouped[:].rearrange("p g n j -> p (g n j)"),
+                in_=grouped[label, t][:].rearrange("p g n j -> p (g n j)"),
             )
-            return codes, scales
+            quantised[label, t] = (codes, scales)
 
-        def times_coefficients(codes, scales, h):
-            cols = slice(h * BANK, (h + 1) * BANK)
-            product = product_banks.tile([P, BANK], F32, tag="product")
-            for g in range(PASSES):
-                nc.tensor.matmul_mx(
-                    out=product[:],
-                    lhsT=codes[:, g, :].bitcast(FP8X4),
-                    lhsT_scale=scales[:, g, :],
-                    rhs=c_codes[:, g, cols].bitcast(FP8X4),
-                    rhs_scale=c_scales[:, g, cols],
-                    start=(g == 0),
-                    stop=(g == PASSES - 1),
-                )
-            return product
-
-        doubled_a, a_quantised, b_plus_a, b_quantised = {}, {}, {}, {}
-
-        def first_argument(t):
-            doubled_a[t] = work.tile([P, H], F32, name="doubled_a")
-            nc.vector.scalar_tensor_tensor(
-                out=doubled_a[t][:], in0=y[t][:], scalar=2.0, in1=k2_rows[t][:], op0=MULT, op1=ADD
-            )
-            a_quantised[t] = quantise_argument(doubled_a[t], 0.5, "a")
-
-        def first_product(t):
-            codes, scales = a_quantised[t]
-            b = work.tile([P, H], F32, name="b")
+        def times_coefficients(label, t):
+            codes, scales = quantised[label, t]
             for h in range(HALVES):
                 cols = slice(h * BANK, (h + 1) * BANK)
-                k3 = times_coefficients(codes, scales, h)
-                nc.vector.tensor_tensor(out=b[:, cols], in0=k3[:], in1=y[t][:, cols], op=ADD)
-            b_quantised[t] = quantise_argument(b, 1.0, "b")
-            b_plus_a[t] = work.tile([P, H], F32, name="b_plus_a")
-            nc.gpsimd.tensor_tensor(out=b_plus_a[t][:], in0=b[:], in1=doubled_a[t][:], op=ADD)
+                product[label, t, h] = product_banks.tile([P, BANK], F32, name="product")
+                for g in range(PASSES):
+                    nc.tensor.matmul_mx(
+                        out=product[label, t, h][:],
+                        lhsT=codes[:, g, :].bitcast(FP8X4),
+                        lhsT_scale=scales[:, g, :],
+                        rhs=c_codes[:, g, cols].bitcast(FP8X4),
+                        rhs_scale=c_scales[:, g, cols],
+                        start=(g == 0),
+                        stop=(g == PASSES - 1),
+                    )
 
-        def second_product(t):
-            k1_sixth = work.tile([P, H], F32, name="k1_sixth")
-            nc.scalar.activation(out=k1_sixth[:], in_=k1_rows[t][:], func=COPY, scale=1.0 / 6.0)
-            from_inputs = work.tile([P, H], F32, name="from_inputs")
+        def compute_second_argument(t):
+            b[t] = work.tile([P, H], F32, name="b")
+            for h in range(HALVES):
+                cols = slice(h * BANK, (h + 1) * BANK)
+                k3 = product["a", t, h]
+                nc.vector.tensor_tensor(out=b[t][:, cols], in0=k3[:], in1=y[t][:, cols], op=ADD)
+
+        def add_arguments(t):
+            b_plus_a[t] = work.tile([P, H], F32, name="b_plus_a")
+            nc.gpsimd.tensor_tensor(out=b_plus_a[t][:], in0=b[t][:], in1=doubled_a[t][:], op=ADD)
+
+        def start_total(t):
+            total[t] = work.tile([P, H], F32, name="total", bufs=OUT_BEHIND + 4)
+            nc.scalar.activation(out=total[t][:], in_=k1_rows[t][:], func=COPY, scale=1.0 / 6.0)
             nc.gpsimd.tensor_tensor(
-                out=from_inputs[:], in0=k1_sixth[:], in1=x_next[t][:], op=SUBTRACT
+                out=total[t][:], in0=total[t][:], in1=x_next[t][:], op=SUBTRACT
             )
-            all_but_k4 = work.tile([P, H], F32, name="all_but_k4")
+
+        def finish_total(t):
             nc.vector.scalar_tensor_tensor(
-                out=all_but_k4[:],
+                out=total[t][:],
                 in0=b_plus_a[t][:],
                 scalar=1.0 / 3.0,
-                in1=from_inputs[:],
+                in1=total[t][:],
                 op0=MULT,
                 op1=ADD,
             )
-            codes, scales = b_quantised[t]
-            result = work.tile([P, H], F32, name="result")
             for h in range(HALVES):
                 cols = slice(h * BANK, (h + 1) * BANK)
-                k4 = times_coefficients(codes, scales, h)
+                k4 = product["b", t, h]
                 nc.vector.scalar_tensor_tensor(
-                    out=result[:, cols],
+                    out=total[t][:, cols],
                     in0=k4[:],
                     scalar=1.0 / 6.0,
-                    in1=all_but_k4[:, cols],
+                    in1=total[t][:, cols],
                     op0=MULT,
                     op1=ADD,
                 )
-                nc.sync.dma_start(out=out[t, :, cols], in_=result[:, cols])
+                nc.sync.dma_start(out=out[t, :, cols], in_=total[t][:, cols])
 
-        for step in range(ROW_TILES + 2):
-            if 0 <= step - 2:
-                second_product(step - 2)
-            if 0 <= step - 1 < ROW_TILES:
-                first_product(step - 1)
-            if step < ROW_TILES:
-                first_argument(step)
+        def exists(t):
+            return 0 <= t < ROW_TILES
+
+        for r in range(-A_AHEAD, ROW_TILES + OUT_BEHIND):
+            if exists(r - OUT_BEHIND):
+                times_coefficients("b", r - OUT_BEHIND)
+            if exists(r):
+                times_coefficients("a", r)
+            if exists(r - B_BEHIND):
+                compute_second_argument(r - B_BEHIND)
+            if exists(r + A_AHEAD):
+                compute_first_argument(r + A_AHEAD)
+            if exists(r - B_BEHIND):
+                turn("b", b[r - B_BEHIND], 1.0, r - B_BEHIND)
+            if exists(r + A_AHEAD):
+                turn("a", doubled_a[r + A_AHEAD], 0.5, r + A_AHEAD)
+            if exists(r - B_BEHIND):
+                add_arguments(r - B_BEHIND)
+            if exists(r + 1):
+                start_total(r + 1)
+            if exists(r - OUT_BEHIND):
+                finish_total(r - OUT_BEHIND)
+            if exists(r - B_BEHIND):
+                quantise("b", r - B_BEHIND)
+            if exists(r + 1):
+                quantise("a", r + 1)

@@ -22,9 +22,7 @@ BANK = 512
 HALVES = H // BANK
 ROW_TILES = 8
 
-A_AHEAD = 2
-B_BEHIND = 1
-OUT_BEHIND = 2
+AHEAD = 2
 
 FLOPS = 2 * 2 * (ROW_TILES * P) * H * H
 
@@ -93,7 +91,7 @@ def tile_sindylossmixin_pa_kernel(tc, x, k1, k2, coefficients, out):
         grouped, quantised, product = {}, {}, {}
 
         def compute_first_argument(t):
-            doubled_a[t] = work.tile([P, H], F32, name="doubled_a", bufs=A_AHEAD + B_BEHIND + 2)
+            doubled_a[t] = work.tile([P, H], F32, name="doubled_a", bufs=AHEAD + 2)
             nc.vector.scalar_tensor_tensor(
                 out=doubled_a[t][:], in0=y[t][:], scalar=2.0, in1=k2_rows[t][:], op0=MULT, op1=ADD
             )
@@ -149,16 +147,18 @@ def tile_sindylossmixin_pa_kernel(tc, x, k1, k2, coefficients, out):
 
         def add_arguments(t):
             b_plus_a[t] = work.tile([P, H], F32, name="b_plus_a")
-            nc.gpsimd.tensor_tensor(out=b_plus_a[t][:], in0=b[t][:], in1=doubled_a[t][:], op=ADD)
+            nc.vector.tensor_tensor(out=b_plus_a[t][:], in0=b[t][:], in1=doubled_a[t][:], op=ADD)
 
         def start_total(t):
-            total[t] = work.tile([P, H], F32, name="total", bufs=OUT_BEHIND + 4)
+            total[t] = work.tile([P, H], F32, name="total", bufs=AHEAD + 4)
             nc.scalar.activation(out=total[t][:], in_=k1_rows[t][:], func=COPY, scale=1.0 / 6.0)
+
+        def subtract_next_state(t):
             nc.gpsimd.tensor_tensor(
                 out=total[t][:], in0=total[t][:], in1=x_next[t][:], op=SUBTRACT
             )
 
-        def finish_total(t):
+        def add_arguments_to_total(t):
             nc.vector.scalar_tensor_tensor(
                 out=total[t][:],
                 in0=b_plus_a[t][:],
@@ -167,6 +167,8 @@ def tile_sindylossmixin_pa_kernel(tc, x, k1, k2, coefficients, out):
                 op0=MULT,
                 op1=ADD,
             )
+
+        def add_k4_and_store(t):
             for h in range(HALVES):
                 cols = slice(h * BANK, (h + 1) * BANK)
                 k4 = product["b", t, h]
@@ -183,26 +185,26 @@ def tile_sindylossmixin_pa_kernel(tc, x, k1, k2, coefficients, out):
         def exists(t):
             return 0 <= t < ROW_TILES
 
-        for r in range(-A_AHEAD, ROW_TILES + OUT_BEHIND):
-            if exists(r - OUT_BEHIND):
-                times_coefficients("b", r - OUT_BEHIND)
-            if exists(r):
-                times_coefficients("a", r)
-            if exists(r - B_BEHIND):
-                compute_second_argument(r - B_BEHIND)
-            if exists(r + A_AHEAD):
-                compute_first_argument(r + A_AHEAD)
-            if exists(r - B_BEHIND):
-                turn("b", b[r - B_BEHIND], 1.0, r - B_BEHIND)
-            if exists(r + A_AHEAD):
-                turn("a", doubled_a[r + A_AHEAD], 0.5, r + A_AHEAD)
-            if exists(r - B_BEHIND):
-                add_arguments(r - B_BEHIND)
+        for r in range(-AHEAD, ROW_TILES + 1):
             if exists(r + 1):
-                start_total(r + 1)
-            if exists(r - OUT_BEHIND):
-                finish_total(r - OUT_BEHIND)
-            if exists(r - B_BEHIND):
-                quantise("b", r - B_BEHIND)
+                subtract_next_state(r + 1)
+            if exists(r):
+                compute_second_argument(r)
+            if exists(r - 1):
+                add_k4_and_store(r - 1)
+            if exists(r):
+                turn("b", b[r], 1.0, r)
+            if exists(r + AHEAD):
+                start_total(r + AHEAD)
             if exists(r + 1):
                 quantise("a", r + 1)
+                times_coefficients("a", r + 1)
+            if exists(r):
+                add_arguments(r)
+                quantise("b", r)
+                times_coefficients("b", r)
+            if exists(r + AHEAD):
+                compute_first_argument(r + AHEAD)
+                turn("a", doubled_a[r + AHEAD], 0.5, r + AHEAD)
+            if exists(r):
+                add_arguments_to_total(r)

@@ -15,6 +15,7 @@ COPY = mybir.ActivationFunctionType.Copy
 
 P = 128
 PACK = 4
+PAIR = 2
 K_PASS = P * PACK
 H = 1024
 PASSES = H // K_PASS
@@ -36,10 +37,8 @@ def tile_sindylossmixin_pa_kernel(tc, x, k1, k2, coefficients, out):
         turned_banks = stack.enter_context(tc.psum_pool(name="turned_banks", bufs=4))
         product_banks = stack.enter_context(tc.psum_pool(name="product_banks", bufs=4))
 
-        identity_bf16 = keep.tile([P, P], BF16)
-        make_identity(nc, identity_bf16[:])
-        identity_f32 = keep.tile([P, P], F32)
-        make_identity(nc, identity_f32[:])
+        identity = keep.tile([P, P], F32)
+        make_identity(nc, identity[:])
 
         y, x_next, k1_rows, k2_rows, c_rows = [], [], [], [], []
         for t in range(ROW_TILES):
@@ -65,52 +64,61 @@ def tile_sindylossmixin_pa_kernel(tc, x, k1, k2, coefficients, out):
             load_rest(t - 1)
         load_rest(ROW_TILES - 1)
 
-        c_grouped = keep.tile([P, PASSES, H, PACK], BF16, align_bytes=64)
+        c_grouped = keep.tile([P, PASSES, H, PAIR], F32, align_bytes=64)
         c_codes = keep.tile([P, PASSES, H], U32, align_bytes=64)
         c_scales = keep.tile([P, PASSES, H], U8, align_bytes=64)
         tiles_per_half = BANK // P
-        for r in range(ROW_TILES):
-            rows = slice(r * P, (r + 1) * P)
-            for g in range(PASSES):
-                turned = turned_banks.tile([P, PACK, P], BF16, tag="turned")
-                for j in range(PACK):
-                    k_cols = slice(g * K_PASS + j * P, g * K_PASS + (j + 1) * P)
-                    nc.tensor.transpose(turned[:, j, :], c_rows[r][:, k_cols], identity_bf16[:])
-                copy_out = nc.vector.tensor_copy if g == 0 else nc.scalar.copy
-                copy_out(out=c_grouped[:, g, rows, :], in_=turned[:].rearrange("p j i -> p i j"))
-            if (r + 1) % tiles_per_half == 0:
-                half = slice((r + 1) * P - BANK, (r + 1) * P)
+
+        def prepare_coefficients():
+            for r in range(ROW_TILES):
+                rows = slice(r * P, (r + 1) * P)
+                words = c_rows[r][:].bitcast(F32)
+                turned = turned_banks.tile([P, PASSES, PAIR, P], F32, tag="turned")
                 for g in range(PASSES):
-                    nc.vector.quantize_mx(
-                        out=c_codes[:, g, half].bitcast(FP8X4),
-                        scales=c_scales[:, g, half],
-                        in_=c_grouped[:, g, half, :].rearrange("p i j -> p (i j)"),
-                    )
+                    for u in range(PAIR):
+                        first = (g * PAIR + u) * P
+                        nc.tensor.transpose(turned[:, g, u, :], words[:, first : first + P], identity[:])
+                copy_out = nc.vector.tensor_copy if r % 2 == 0 else nc.scalar.copy
+                copy_out(out=c_grouped[:, :, rows, :], in_=turned[:].rearrange("p g u i -> p g i u"))
+                if (r + 1) % tiles_per_half == 0:
+                    half = slice((r + 1) * P - BANK, (r + 1) * P)
+                    for g in range(PASSES):
+                        nc.vector.quantize_mx(
+                            out=c_codes[:, g, half].bitcast(FP8X4),
+                            scales=c_scales[:, g, half],
+                            in_=c_grouped[:, g, half, :].rearrange("p i u -> p (i u)").bitcast(BF16),
+                        )
 
         doubled_a, b, b_plus_a, total = {}, {}, {}, {}
         grouped, quantised, product = {}, {}, {}
-
-        def compute_first_argument(t):
-            doubled_a[t] = work.tile([P, H], F32, name="doubled_a", bufs=AHEAD + 2)
-            nc.vector.scalar_tensor_tensor(
-                out=doubled_a[t][:], in0=y[t][:], scalar=2.0, in1=k2_rows[t][:], op0=MULT, op1=ADD
-            )
 
         def turn(label, argument, scale, t):
             grouped[label, t] = work.tile(
                 [P, PASSES, P, PACK], BF16, name="grouped_" + label, align_bytes=64
             )
+            columns = argument[:].rearrange(
+                "n (g u q e) -> n g u e q", g=PASSES, u=PAIR, q=P, e=PAIR
+            )
             for g in range(PASSES):
                 turned = turned_banks.tile([P, PACK, P], F32, tag="turned")
-                for j in range(PACK):
-                    k_cols = slice(g * K_PASS + j * P, g * K_PASS + (j + 1) * P)
-                    nc.tensor.transpose(turned[:, j, :], argument[:, k_cols], identity_f32[:])
+                for u in range(PAIR):
+                    for e in range(PAIR):
+                        nc.tensor.transpose(
+                            turned[:, PAIR * u + e, :], columns[:, g, u, e, :], identity[:]
+                        )
                 nc.scalar.activation(
                     out=grouped[label, t][:, g, :, :],
                     in_=turned[:].rearrange("p j n -> p n j"),
                     func=COPY,
                     scale=scale,
                 )
+
+        def first_argument(t):
+            doubled_a[t] = work.tile([P, H], F32, name="doubled_a", bufs=AHEAD + 2)
+            nc.vector.scalar_tensor_tensor(
+                out=doubled_a[t][:], in0=y[t][:], scalar=2.0, in1=k2_rows[t][:], op0=MULT, op1=ADD
+            )
+            turn("a", doubled_a[t], 0.5, t)
 
         def quantise(label, t):
             codes = work.tile([P, PASSES, P], U32, name="codes_" + label, align_bytes=64)
@@ -150,7 +158,7 @@ def tile_sindylossmixin_pa_kernel(tc, x, k1, k2, coefficients, out):
             nc.vector.tensor_tensor(out=b_plus_a[t][:], in0=b[t][:], in1=doubled_a[t][:], op=ADD)
 
         def start_total(t):
-            total[t] = work.tile([P, H], F32, name="total", bufs=AHEAD + 4)
+            total[t] = work.tile([P, H], F32, name="total", bufs=5)
             nc.scalar.activation(out=total[t][:], in_=k1_rows[t][:], func=COPY, scale=1.0 / 6.0)
 
         def subtract_next_state(t):
@@ -185,17 +193,19 @@ def tile_sindylossmixin_pa_kernel(tc, x, k1, k2, coefficients, out):
         def exists(t):
             return 0 <= t < ROW_TILES
 
-        for r in range(-AHEAD, ROW_TILES + 1):
-            if exists(r + 1):
-                subtract_next_state(r + 1)
+        first_argument(0)
+        prepare_coefficients()
+        for r in range(1 - AHEAD, ROW_TILES + 1):
+            if exists(r):
+                subtract_next_state(r)
             if exists(r):
                 compute_second_argument(r)
             if exists(r - 1):
                 add_k4_and_store(r - 1)
             if exists(r):
                 turn("b", b[r], 1.0, r)
-            if exists(r + AHEAD):
-                start_total(r + AHEAD)
+            if exists(r + 1):
+                start_total(r + 1)
             if exists(r + 1):
                 quantise("a", r + 1)
                 times_coefficients("a", r + 1)
@@ -204,7 +214,6 @@ def tile_sindylossmixin_pa_kernel(tc, x, k1, k2, coefficients, out):
                 quantise("b", r)
                 times_coefficients("b", r)
             if exists(r + AHEAD):
-                compute_first_argument(r + AHEAD)
-                turn("a", doubled_a[r + AHEAD], 0.5, r + AHEAD)
+                first_argument(r + AHEAD)
             if exists(r):
                 add_arguments_to_total(r)

from contextlib import ExitStack

import concourse.mybir as mybir
from concourse.masks import make_identity

BF16 = mybir.dt.bfloat16
F32 = mybir.dt.float32
U32 = mybir.dt.uint32
U8 = mybir.dt.uint8
FP8X4 = mybir.dt.float8_e4m3fn_x4
ADD = mybir.AluOpType.add
SUBTRACT = mybir.AluOpType.subtract
MULT = mybir.AluOpType.mult
COPY = mybir.ActivationFunctionType.Copy

P = 128
PACK = 4
PAIR = 2
K_PASS = P * PACK
H = 1024
PASSES = H // K_PASS
BANK = 512
HALVES = H // BANK
ROW_TILES = 8

AHEAD = 2

FLOPS = 2 * 2 * (ROW_TILES * P) * H * H


def tile_sindylossmixin_pa_kernel(tc, x, k1, k2, coefficients, out):
    nc = tc.nc
    with ExitStack() as stack:
        stack.enter_context(tc.manual_schedule())
        keep = stack.enter_context(tc.tile_pool(name="keep", bufs=1))
        work = stack.enter_context(tc.tile_pool(name="work", bufs=3))
        turned_banks = stack.enter_context(tc.psum_pool(name="turned_banks", bufs=4))
        product_banks = stack.enter_context(tc.psum_pool(name="product_banks", bufs=4))

        identity = keep.tile([P, P], F32)
        make_identity(nc, identity[:])

        y, x_next, k1_rows, k2_rows, c_rows = [], [], [], [], []
        for t in range(ROW_TILES):
            y.append(keep.tile([P, H], BF16, name="y%d" % t))
            x_next.append(keep.tile([P, H], BF16, name="x_next%d" % t))
            k1_rows.append(keep.tile([P, H], BF16, name="k1_rows%d" % t))
            k2_rows.append(keep.tile([P, H], BF16, name="k2_rows%d" % t))
            c_rows.append(keep.tile([P, H], BF16, name="c_rows%d" % t))

        def load_first_argument(t):
            nc.sync.dma_start(out=y[t][:], in_=x[t, 0:P, :])
            nc.sync.dma_start(out=k2_rows[t][:], in_=k2[t * P : (t + 1) * P, :])

        def load_rest(t):
            nc.sync.dma_start(out=k1_rows[t][:], in_=k1[t * P : (t + 1) * P, :])
            nc.sync.dma_start(out=x_next[t][:], in_=x[t, 1 : P + 1, :])

        load_first_argument(0)
        for r in range(ROW_TILES):
            nc.sync.dma_start(out=c_rows[r][:], in_=coefficients[r * P : (r + 1) * P, :])
        for t in range(1, ROW_TILES):
            load_first_argument(t)
            load_rest(t - 1)
        load_rest(ROW_TILES - 1)

        c_grouped = keep.tile([P, PASSES, H, PAIR], F32, align_bytes=64)
        c_codes = keep.tile([P, PASSES, H], U32, align_bytes=64)
        c_scales = keep.tile([P, PASSES, H], U8, align_bytes=64)
        tiles_per_half = BANK // P

        def prepare_coefficients():
            for r in range(ROW_TILES):
                rows = slice(r * P, (r + 1) * P)
                words = c_rows[r][:].bitcast(F32)
                turned = turned_banks.tile([P, PASSES, PAIR, P], F32, tag="turned")
                for g in range(PASSES):
                    for u in range(PAIR):
                        first = (g * PAIR + u) * P
                        nc.tensor.transpose(turned[:, g, u, :], words[:, first : first + P], identity[:])
                copy_out = nc.vector.tensor_copy if r % 2 == 0 else nc.scalar.copy
                copy_out(out=c_grouped[:, :, rows, :], in_=turned[:].rearrange("p g u i -> p g i u"))
                if (r + 1) % tiles_per_half == 0:
                    half = slice((r + 1) * P - BANK, (r + 1) * P)
                    for g in range(PASSES):
                        nc.vector.quantize_mx(
                            out=c_codes[:, g, half].bitcast(FP8X4),
                            scales=c_scales[:, g, half],
                            in_=c_grouped[:, g, half, :].rearrange("p i u -> p (i u)").bitcast(BF16),
                        )

        doubled_a, b, b_plus_a, total = {}, {}, {}, {}
        grouped, quantised, product = {}, {}, {}

        def turn(label, argument, scale, t):
            grouped[label, t] = work.tile(
                [P, PASSES, P, PACK], BF16, name="grouped_" + label, align_bytes=64
            )
            columns = argument[:].rearrange(
                "n (g u q e) -> n g u e q", g=PASSES, u=PAIR, q=P, e=PAIR
            )
            for g in range(PASSES):
                turned = turned_banks.tile([P, PACK, P], F32, tag="turned")
                for u in range(PAIR):
                    for e in range(PAIR):
                        nc.tensor.transpose(
                            turned[:, PAIR * u + e, :], columns[:, g, u, e, :], identity[:]
                        )
                nc.scalar.activation(
                    out=grouped[label, t][:, g, :, :],
                    in_=turned[:].rearrange("p j n -> p n j"),
                    func=COPY,
                    scale=scale,
                )

        def first_argument(t):
            doubled_a[t] = work.tile([P, H], F32, name="doubled_a", bufs=AHEAD + 2)
            nc.vector.scalar_tensor_tensor(
                out=doubled_a[t][:], in0=y[t][:], scalar=2.0, in1=k2_rows[t][:], op0=MULT, op1=ADD
            )
            turn("a", doubled_a[t], 0.5, t)

        def quantise(label, t):
            codes = work.tile([P, PASSES, P], U32, name="codes_" + label, align_bytes=64)
            scales = work.tile([P, PASSES, P], U8, name="scales_" + label, align_bytes=64)
            nc.vector.quantize_mx(
                out=codes[:].rearrange("p g n -> p (g n)").bitcast(FP8X4),
                scales=scales[:].rearrange("p g n -> p (g n)"),
                in_=grouped[label, t][:].rearrange("p g n j -> p (g n j)"),
            )
            quantised[label, t] = (codes, scales)

        def times_coefficients(label, t):
            codes, scales = quantised[label, t]
            for h in range(HALVES):
                cols = slice(h * BANK, (h + 1) * BANK)
                product[label, t, h] = product_banks.tile([P, BANK], F32, name="product")
                for g in range(PASSES):
                    nc.tensor.matmul_mx(
                        out=product[label, t, h][:],
                        lhsT=codes[:, g, :].bitcast(FP8X4),
                        lhsT_scale=scales[:, g, :],
                        rhs=c_codes[:, g, cols].bitcast(FP8X4),
                        rhs_scale=c_scales[:, g, cols],
                        start=(g == 0),
                        stop=(g == PASSES - 1),
                    )

        def compute_second_argument(t):
            b[t] = work.tile([P, H], F32, name="b")
            for h in range(HALVES):
                cols = slice(h * BANK, (h + 1) * BANK)
                k3 = product["a", t, h]
                nc.vector.tensor_tensor(out=b[t][:, cols], in0=k3[:], in1=y[t][:, cols], op=ADD)

        def add_arguments(t):
            b_plus_a[t] = work.tile([P, H], F32, name="b_plus_a")
            nc.vector.tensor_tensor(out=b_plus_a[t][:], in0=b[t][:], in1=doubled_a[t][:], op=ADD)

        def start_total(t):
            total[t] = work.tile([P, H], F32, name="total", bufs=5)
            nc.scalar.activation(out=total[t][:], in_=k1_rows[t][:], func=COPY, scale=1.0 / 6.0)

        def subtract_next_state(t):
            nc.gpsimd.tensor_tensor(
                out=total[t][:], in0=total[t][:], in1=x_next[t][:], op=SUBTRACT
            )

        def add_arguments_to_total(t):
            nc.vector.scalar_tensor_tensor(
                out=total[t][:],
                in0=b_plus_a[t][:],
                scalar=1.0 / 3.0,
                in1=total[t][:],
                op0=MULT,
                op1=ADD,
            )

        def add_k4_and_store(t):
            for h in range(HALVES):
                cols = slice(h * BANK, (h + 1) * BANK)
                k4 = product["b", t, h]
                nc.vector.scalar_tensor_tensor(
                    out=total[t][:, cols],
                    in0=k4[:],
                    scalar=1.0 / 6.0,
                    in1=total[t][:, cols],
                    op0=MULT,
                    op1=ADD,
                )
                nc.sync.dma_start(out=out[t, :, cols], in_=total[t][:, cols])

        def exists(t):
            return 0 <= t < ROW_TILES

        first_argument(0)
        prepare_coefficients()
        for r in range(1 - AHEAD, ROW_TILES + 1):
            if exists(r):
                subtract_next_state(r)
            if exists(r):
                compute_second_argument(r)
            if exists(r - 1):
                add_k4_and_store(r - 1)
            if exists(r):
                turn("b", b[r], 1.0, r)
            if exists(r + 1):
                start_total(r + 1)
            if exists(r + 1):
                quantise("a", r + 1)
                times_coefficients("a", r + 1)
            if exists(r):
                add_arguments(r)
                quantise("b", r)
                times_coefficients("b", r)
            if exists(r + AHEAD):
                first_argument(r + AHEAD)
            if exists(r):
                add_arguments_to_total(r)
